import numpy as np
import ml_dtypes


def mxq(x, axis, fmt="e4m3"):
    dtype, down = {"e4m3": (ml_dtypes.float8_e4m3fn, 7), "e5m2": (ml_dtypes.float8_e5m2, 14)}[fmt]
    v = np.moveaxis(np.asarray(x, np.float32).astype(ml_dtypes.bfloat16).astype(np.float64), axis, -1)
    blocks = v.reshape(v.shape[:-1] + (-1, 32))
    amax = np.abs(blocks).max(-1, keepdims=True)
    byte = np.maximum(np.where(amax > 0, np.frexp(amax)[1] - 1 + 127, 0) - down, 1)
    scale = np.exp2(byte - 127.0)
    codes = (blocks / scale).astype(np.float32).astype(dtype).astype(np.float64)
    return np.moveaxis((codes * scale).reshape(v.shape), -1, axis)


WIDE = False


def mx_kscale(k):
    if not WIDE:
        return np.ones(k)
    levels = np.array([30, -30])
    if k % 512:
        return np.exp2(np.random.permutation(np.resize(levels, k // 32))).repeat(32)
    a = np.empty((k // 512, 16))
    for p in range(k // 512):
        a[p, :8] = np.random.permutation(np.resize(levels, 8))
        for g in range(8):
            far = levels[np.abs(levels - a[p, g]) >= 10]
            a[p, g + 8] = far[np.random.randint(len(far))]
    return np.exp2(a.ravel()).repeat(32)


BF16 = ml_dtypes.bfloat16


def bf(x):
    return np.asarray(x, np.float32).astype(BF16)


def f64(x):
    return np.asarray(x).astype(np.float64)


B, S, H, O, W = 8, 2048, 512, 128, 8


def setup_inputs():
    s = mx_kscale(H)
    return {"hidden_states": bf(np.random.standard_normal((B, S, H)) * s),
            "gate_proj": bf(np.random.standard_normal((O, H)) / np.sqrt(H) / s[None, :]),
            "world_size": W}


def reference(hidden_states, gate_proj, world_size):
    h = gate_proj.shape[1]
    view = f64(hidden_states).reshape(-1, h)
    mm = mxq(view, 1, "e5m2") @ mxq(f64(gate_proj), 1, "e4m3").T
    n, o = mm.shape
    out = mm.reshape(world_size, n // world_size, o).sum(axis=0)
    return out

@@ -1,0 +1,207 @@
+from contextlib import ExitStack
+
+import concourse.mybir as mybir
+from concourse.masks import make_identity
+
+FLOPS = 2 * 16384 * 512 * 128
+
+F32 = mybir.dt.float32
+BF16 = mybir.dt.bfloat16
+U32 = mybir.dt.uint32
+U8 = mybir.dt.uint8
+E5M2X4 = mybir.dt.float8_e5m2_x4
+E4M3X4 = mybir.dt.float8_e4m3fn_x4
+
+P = 128
+RANKS = 8
+ROWS = 2048
+CHUNK = 512
+SUB = CHUNK // P
+NJ = ROWS // CHUNK
+NCH = NJ * RANKS
+LAG = 2
+
+
+def is_perm(c):
+    return False
+
+
+def evac_engine(c, b):
+    return "V" if (b == 1 and c % 2 == 1) else "S"
+
+
+def tile_testmmrsmodel_t_kernel(tc, hidden_states, gate_proj, world_size, out):
+    nc = tc.nc
+    assert world_size == RANKS
+    view = hidden_states.flatten_outer_dims()
+
+    with ExitStack() as ctx:
+        keep = ctx.enter_context(tc.tile_pool(name="keep", bufs=1))
+        work = ctx.enter_context(tc.tile_pool(name="work", bufs=3))
+        psum_t = ctx.enter_context(tc.psum_pool(name="psum_t", bufs=6))
+        psum_a = ctx.enter_context(tc.psum_pool(name="psum_a", bufs=2))
+        ctx.enter_context(tc.manual_schedule())
+
+        x = {}
+        pw = {}
+        tp = {}
+        gq = {}
+        codes = {}
+        scales = {}
+        acc = {}
+        acc_sb = {}
+        tpo = {}
+
+        warm_in = keep.tile([P, 1], F32, name="warm_in", tag="warm_in")
+        warm_out = keep.tile([P, 1], F32, name="warm_out", tag="warm_out")
+        nc.vector.memset(warm_in[:], 0.0)
+        nc.scalar.copy(out=warm_out[:], in_=warm_in[:])
+
+        ident = keep.tile([P, P], F32, name="ident", tag="ident")
+        make_identity(nc, ident[:])
+
+        gate_sb = keep.tile([P, 512], BF16, name="gate_sb", tag="gate_sb")
+        nc.sync.dma_start(out=gate_sb[:], in_=gate_proj)
+        for c in range(NCH):
+            row0 = (c % RANKS) * ROWS + (c // RANKS) * CHUNK
+            xt = keep.tile([P, SUB * 512], BF16, name="x%d" % c, tag="x%d" % c)
+            nc.sync.dma_start(
+                out=xt[:],
+                in_=view[row0 : row0 + CHUNK, :].rearrange("(p i) k -> p (i k)", i=SUB),
+            )
+            x[c] = xt
+
+        gate_w = gate_sb[:].bitcast(F32)
+        tg = psum_t.tile([P, 2, 2, P], F32, name="tg", tag="tp")
+        for u in range(2):
+            nc.tensor.transpose(tg[:, 0, u, :], gate_w[:, u:256:2], ident[:])
+        gate_q = keep.tile([P, P, 4], BF16, name="gate_q", tag="gate_q", align_bytes=64)
+        nc.vector.tensor_copy(
+            out=gate_q[:].bitcast(F32), in_=tg[:, 0, :, :].rearrange("m u o -> m o u")
+        )
+        gate_codes = keep.tile([P, P], U32, name="gate_codes", tag="gate_codes", align_bytes=64)
+        gate_scales = keep.tile([P, P], U8, name="gate_scales", tag="gate_scales", align_bytes=64)
+        nc.vector.quantize_mx(
+            out=gate_codes[:].bitcast(E4M3X4),
+            scales=gate_scales[:],
+            in_=gate_q[:].rearrange("m o t -> m (o t)"),
+        )
+
+        def perm(c):
+            t = work.tile([P, 2, SUB, P], F32, name="pw", tag="pw", bufs=4)
+            nc.vector.tensor_copy(
+                out=t[:],
+                in_=x[c][:].bitcast(F32).rearrange("p (i m u) -> p u i m", i=SUB, u=2),
+            )
+            pw[c] = t
+
+        def trans(c):
+            xw = x[c][:].bitcast(F32)
+            banks = []
+            for b in range(2):
+                t = psum_t.tile([P, 2, 2, P], F32, name="tp", tag="tp")
+                for a in range(2):
+                    i = 2 * b + a
+                    for u in range(2):
+                        if is_perm(c):
+                            src = pw[c][:, u, i, :]
+                        else:
+                            src = xw[:, i * 256 + u : (i + 1) * 256 : 2]
+                        nc.tensor.transpose(t[:, a, u, :], src, ident[:])
+                banks.append(t)
+            tp[c] = banks
+
+        def evac(c, eng):
+            if c not in gq:
+                gq[c] = work.tile([P, SUB, P, 4], BF16, name="gq", tag="gq", bufs=4, align_bytes=64)
+            gw = gq[c][:].bitcast(F32)
+            for b in range(2):
+                if evac_engine(c, b) != eng:
+                    continue
+                dst = gw[:, 2 * b : 2 * b + 2, :, :]
+                src = tp[c][b][:].rearrange("m a u p -> m a p u")
+                if eng == "S":
+                    nc.scalar.copy(out=dst, in_=src)
+                else:
+                    nc.vector.tensor_copy(out=dst, in_=src)
+
+        def quant(c):
+            cd = work.tile([P, CHUNK], U32, name="codes", tag="codes", bufs=6, align_bytes=64)
+            sc = work.tile([P, CHUNK], U8, name="scales", tag="scales", bufs=6, align_bytes=64)
+            nc.vector.quantize_mx(
+                out=cd[:].bitcast(E5M2X4),
+                scales=sc[:],
+                in_=gq[c][:].rearrange("m i p t -> m (i p t)"),
+            )
+            codes[c] = cd
+            scales[c] = sc
+
+        def mm(c):
+            jt = c // RANKS
+            r = c % RANKS
+            if r == 0:
+                acc[jt] = psum_a.tile([P, CHUNK], F32, name="acc", tag="acc")
+            nc.tensor.matmul_mx(
+                out=acc[jt][:],
+                lhsT=gate_codes[:].bitcast(E4M3X4),
+                lhsT_scale=gate_scales[:],
+                rhs=codes[c][:].bitcast(E5M2X4),
+                rhs_scale=scales[c][:],
+                start=(r == 0),
+                stop=(r == RANKS - 1),
+            )
+
+        def epi_acc(jt):
+            t = work.tile([P, CHUNK], F32, name="acc_sb", tag="acc_sb", bufs=2)
+            nc.vector.tensor_copy(out=t[:], in_=acc[jt][:])
+            acc_sb[jt] = t
+
+        def epi_trans(jt):
+            t = psum_t.tile([P, SUB, P], F32, name="tpo", tag="tp")
+            for i in range(SUB):
+                nc.tensor.transpose(t[:, i, :], acc_sb[jt][:, i * P : (i + 1) * P], ident[:])
+            tpo[jt] = t
+
+        def epi_out(jt):
+            t = work.tile([P, SUB, P], F32, name="out_sb", tag="out_sb", bufs=2)
+            nc.scalar.copy(out=t[:], in_=tpo[jt][:])
+            dst = out[jt * CHUNK : (jt + 1) * CHUNK, :].rearrange("(p i) o -> p i o", i=SUB)
+            nc.scalar.dma_start(out=dst, in_=t[:])
+
+        at_acc = {}
+        at_trans = {}
+        at_out = {}
+        for s in range(-3, NCH + LAG):
+            odd = s % 2 == 1
+            if odd:
+                for c in (s + 1, s + 2):
+                    if 0 <= c < NCH:
+                        trans(c)
+                for jt in at_trans.get(s, []):
+                    epi_trans(jt)
+            if 0 <= s + 1 < NCH:
+                evac(s + 1, "S")
+            for jt in at_out.get(s, []):
+                epi_out(jt)
+            if 0 <= s < NCH:
+                quant(s)
+            if 0 <= s + 1 < NCH:
+                evac(s + 1, "V")
+            for jt in at_acc.get(s, []):
+                epi_acc(jt)
+            if 0 <= s + 3 < NCH and is_perm(s + 3):
+                perm(s + 3)
+            if odd:
+                for c in (s - 1 - LAG, s - LAG):
+                    if 0 <= c < NCH:
+                        mm(c)
+                        if c % RANKS == RANKS - 1:
+                            jt = c // RANKS
+                            if jt == NJ - 1:
+                                epi_acc(jt)
+                                epi_trans(jt)
+                                epi_out(jt)
+                            else:
+                                at_acc[s + 1] = [jt]
+                                at_trans[s + 2] = [jt]
+                                at_out[s + 3] = [jt]

@@ -23,11 +23,11 @@ LAG = 2
 
 
 def is_perm(c):
-    return False
+    return 2 <= c < NCH - 1 and c % 4 != 3
 
 
 def evac_engine(c, b):
-    return "V" if (b == 1 and c % 2 == 1) else "S"
+    return "V" if (b == 1 and (c < 2 or c == NCH - 1)) else "S"
 
 
 def tile_testmmrsmodel_t_kernel(tc, hidden_states, gate_proj, world_size, out):

@@ -19,15 +19,18 @@ CHUNK = 512
 SUB = CHUNK // P
 NJ = ROWS // CHUNK
 NCH = NJ * RANKS
-LAG = 2
+LAG = 4
+PLEAD = 4
+TLEAD = 2
+GROUP = 2
 
 
 def is_perm(c):
-    return 2 <= c < NCH - 1 and c % 4 != 3
+    return c >= 8 and c % 2 == 0
 
 
 def evac_engine(c, b):
-    return "V" if (b == 1 and (c < 2 or c == NCH - 1)) else "S"
+    return "V" if (b == 1 and (c % 4 == 0 or c == NCH - 1)) else "S"
 
 
 def tile_testmmrsmodel_t_kernel(tc, hidden_states, gate_proj, world_size, out):
@@ -88,7 +91,7 @@ def tile_testmmrsmodel_t_kernel(tc, hidden_states, gate_proj, world_size, out):
         )
 
         def perm(c):
-            t = work.tile([P, 2, SUB, P], F32, name="pw", tag="pw", bufs=4)
+            t = work.tile([P, 2, SUB, P], F32, name="pw", tag="pw", bufs=6)
             nc.vector.tensor_copy(
                 out=t[:],
                 in_=x[c][:].bitcast(F32).rearrange("p (i m u) -> p u i m", i=SUB, u=2),
@@ -126,8 +129,8 @@ def tile_testmmrsmodel_t_kernel(tc, hidden_states, gate_proj, world_size, out):
                     nc.vector.tensor_copy(out=dst, in_=src)
 
         def quant(c):
-            cd = work.tile([P, CHUNK], U32, name="codes", tag="codes", bufs=6, align_bytes=64)
-            sc = work.tile([P, CHUNK], U8, name="scales", tag="scales", bufs=6, align_bytes=64)
+            cd = work.tile([P, CHUNK], U32, name="codes", tag="codes", bufs=8, align_bytes=64)
+            sc = work.tile([P, CHUNK], U8, name="scales", tag="scales", bufs=8, align_bytes=64)
             nc.vector.quantize_mx(
                 out=cd[:].bitcast(E5M2X4),
                 scales=sc[:],
@@ -171,37 +174,38 @@ def tile_testmmrsmodel_t_kernel(tc, hidden_states, gate_proj, world_size, out):
         at_acc = {}
         at_trans = {}
         at_out = {}
-        for s in range(-3, NCH + LAG):
-            odd = s % 2 == 1
-            if odd:
-                for c in (s + 1, s + 2):
-                    if 0 <= c < NCH:
-                        trans(c)
-                for jt in at_trans.get(s, []):
-                    epi_trans(jt)
+        state = {"next_mm": 0}
+        for s in range(-PLEAD, NCH + LAG + GROUP):
+            if 0 <= s + TLEAD < NCH:
+                trans(s + TLEAD)
+            for jt in at_trans.get(s, []):
+                epi_trans(jt)
             if 0 <= s + 1 < NCH:
                 evac(s + 1, "S")
             for jt in at_out.get(s, []):
                 epi_out(jt)
-            if 0 <= s < NCH:
-                quant(s)
             if 0 <= s + 1 < NCH:
                 evac(s + 1, "V")
+            if 0 <= s < NCH:
+                quant(s)
             for jt in at_acc.get(s, []):
                 epi_acc(jt)
-            if 0 <= s + 3 < NCH and is_perm(s + 3):
-                perm(s + 3)
-            if odd:
-                for c in (s - 1 - LAG, s - LAG):
-                    if 0 <= c < NCH:
-                        mm(c)
-                        if c % RANKS == RANKS - 1:
-                            jt = c // RANKS
-                            if jt == NJ - 1:
-                                epi_acc(jt)
-                                epi_trans(jt)
-                                epi_out(jt)
-                            else:
-                                at_acc[s + 1] = [jt]
-                                at_trans[s + 2] = [jt]
-                                at_out[s + 3] = [jt]
+            if 0 <= s + PLEAD < NCH and is_perm(s + PLEAD):
+                perm(s + PLEAD)
+            draining = s + TLEAD >= NCH - 1
+            if draining or (s + 1) % GROUP == 0:
+                hi = min(NCH - 1, s if draining else s - LAG)
+                while state["next_mm"] <= hi:
+                    c = state["next_mm"]
+                    state["next_mm"] = c + 1
+                    mm(c)
+                    if c % RANKS == RANKS - 1:
+                        jt = c // RANKS
+                        if jt == NJ - 1:
+                            epi_acc(jt)
+                            epi_trans(jt)
+                            epi_out(jt)
+                        else:
+                            at_acc[s + 1] = [jt]
+                            at_trans[s + 2] = [jt]
+                            at_out[s + 3] = [jt]

@@ -26,7 +26,7 @@ GROUP = 2
 
 
 def is_perm(c):
-    return c >= 8 and c % 2 == 0
+    return c >= 8 and (c % 2 == 0 or c == NCH - 1)
 
 
 def evac_engine(c, b):
@@ -64,7 +64,6 @@ def tile_testmmrsmodel_t_kernel(tc, hidden_states, gate_proj, world_size, out):
         make_identity(nc, ident[:])
 
         gate_sb = keep.tile([P, 512], BF16, name="gate_sb", tag="gate_sb")
-        nc.sync.dma_start(out=gate_sb[:], in_=gate_proj)
         for c in range(NCH):
             row0 = (c % RANKS) * ROWS + (c // RANKS) * CHUNK
             xt = keep.tile([P, SUB * 512], BF16, name="x%d" % c, tag="x%d" % c)
@@ -73,22 +72,30 @@ def tile_testmmrsmodel_t_kernel(tc, hidden_states, gate_proj, world_size, out):
                 in_=view[row0 : row0 + CHUNK, :].rearrange("(p i) k -> p (i k)", i=SUB),
             )
             x[c] = xt
+            if c == 1:
+                nc.sync.dma_start(out=gate_sb[:], in_=gate_proj)
 
-        gate_w = gate_sb[:].bitcast(F32)
-        tg = psum_t.tile([P, 2, 2, P], F32, name="tg", tag="tp")
-        for u in range(2):
-            nc.tensor.transpose(tg[:, 0, u, :], gate_w[:, u:256:2], ident[:])
         gate_q = keep.tile([P, P, 4], BF16, name="gate_q", tag="gate_q", align_bytes=64)
-        nc.vector.tensor_copy(
-            out=gate_q[:].bitcast(F32), in_=tg[:, 0, :, :].rearrange("m u o -> m o u")
-        )
         gate_codes = keep.tile([P, P], U32, name="gate_codes", tag="gate_codes", align_bytes=64)
         gate_scales = keep.tile([P, P], U8, name="gate_scales", tag="gate_scales", align_bytes=64)
-        nc.vector.quantize_mx(
-            out=gate_codes[:].bitcast(E4M3X4),
-            scales=gate_scales[:],
-            in_=gate_q[:].rearrange("m o t -> m (o t)"),
-        )
+        gate_bank = {}
+
+        def gate_trans():
+            gate_w = gate_sb[:].bitcast(F32)
+            tg = psum_t.tile([P, 2, 2, P], F32, name="tg", tag="tp")
+            for u in range(2):
+                nc.tensor.transpose(tg[:, 0, u, :], gate_w[:, u:256:2], ident[:])
+            gate_bank[0] = tg
+
+        def gate_quant():
+            nc.vector.tensor_copy(
+                out=gate_q[:].bitcast(F32), in_=gate_bank[0][:, 0, :, :].rearrange("m u o -> m o u")
+            )
+            nc.vector.quantize_mx(
+                out=gate_codes[:].bitcast(E4M3X4),
+                scales=gate_scales[:],
+                in_=gate_q[:].rearrange("m o t -> m (o t)"),
+            )
 
         def perm(c):
             t = work.tile([P, 2, SUB, P], F32, name="pw", tag="pw", bufs=6)
@@ -171,6 +178,26 @@ def tile_testmmrsmodel_t_kernel(tc, hidden_states, gate_proj, world_size, out):
             dst = out[jt * CHUNK : (jt + 1) * CHUNK, :].rearrange("(p i) o -> p i o", i=SUB)
             nc.scalar.dma_start(out=dst, in_=t[:])
 
+        def epi_last(jt):
+            dst = out[jt * CHUNK : (jt + 1) * CHUNK, :].rearrange("(p i) o -> p i o", i=SUB)
+            halves = []
+            for h in range(2):
+                a = work.tile([P, 2 * P], F32, name="acc_h%d" % h, tag="acc_h%d" % h, bufs=1)
+                nc.vector.tensor_copy(out=a[:], in_=acc[jt][:, h * 2 * P : (h + 1) * 2 * P])
+                halves.append(a)
+            banks = []
+            for h in range(2):
+                t = psum_t.tile([P, 2, P], F32, name="tpo_h", tag="tp")
+                for i in range(2):
+                    nc.tensor.transpose(t[:, i, :], halves[h][:, i * P : (i + 1) * P], ident[:])
+                banks.append(t)
+            o0 = work.tile([P, 2, P], F32, name="out_h0", tag="out_h0", bufs=1)
+            nc.scalar.copy(out=o0[:], in_=banks[0][:])
+            nc.scalar.dma_start(out=dst[:, 0:2, :], in_=o0[:])
+            o1 = work.tile([P, 2, P], F32, name="out_h1", tag="out_h1", bufs=1)
+            nc.vector.tensor_copy(out=o1[:], in_=banks[1][:])
+            nc.sync.dma_start(out=dst[:, 2:4, :], in_=o1[:])
+
         at_acc = {}
         at_trans = {}
         at_out = {}
@@ -178,6 +205,8 @@ def tile_testmmrsmodel_t_kernel(tc, hidden_states, gate_proj, world_size, out):
         for s in range(-PLEAD, NCH + LAG + GROUP):
             if 0 <= s + TLEAD < NCH:
                 trans(s + TLEAD)
+            if s + TLEAD == 1:
+                gate_trans()
             for jt in at_trans.get(s, []):
                 epi_trans(jt)
             if 0 <= s + 1 < NCH:
@@ -186,6 +215,8 @@ def tile_testmmrsmodel_t_kernel(tc, hidden_states, gate_proj, world_size, out):
                 epi_out(jt)
             if 0 <= s + 1 < NCH:
                 evac(s + 1, "V")
+            if s + TLEAD == 1:
+                gate_quant()
             if 0 <= s < NCH:
                 quant(s)
             for jt in at_acc.get(s, []):
@@ -202,9 +233,7 @@ def tile_testmmrsmodel_t_kernel(tc, hidden_states, gate_proj, world_size, out):
                     if c % RANKS == RANKS - 1:
                         jt = c // RANKS
                         if jt == NJ - 1:
-                            epi_acc(jt)
-                            epi_trans(jt)
-                            epi_out(jt)
+                            epi_last(jt)
                         else:
                             at_acc[s + 1] = [jt]
                             at_trans[s + 2] = [jt]

@@ -26,11 +26,11 @@ GROUP = 2
 
 
 def is_perm(c):
-    return c >= 8 and (c % 2 == 0 or c == NCH - 1)
+    return c >= 8 and (c % 2 == 0 or c % 6 == 1)
 
 
 def evac_engine(c, b):
-    return "V" if (b == 1 and (c % 4 == 0 or c == NCH - 1)) else "S"
+    return "V" if (b == 1 and (c % 8 == 0 or c == NCH - 1)) else "S"
 
 
 def tile_testmmrsmodel_t_kernel(tc, hidden_states, gate_proj, world_size, out):

@@ -163,7 +163,10 @@ def tile_testmmrsmodel_t_kernel(tc, hidden_states, gate_proj, world_size, out):
 
         def epi_acc(jt):
             t = work.tile([P, CHUNK], F32, name="acc_sb", tag="acc_sb", bufs=2)
-            nc.vector.tensor_copy(out=t[:], in_=acc[jt][:])
+            if jt == NJ - 2:
+                nc.scalar.copy(out=t[:], in_=acc[jt][:])
+            else:
+                nc.vector.tensor_copy(out=t[:], in_=acc[jt][:])
             acc_sb[jt] = t
 
         def epi_trans(jt):
@@ -185,6 +188,8 @@ def tile_testmmrsmodel_t_kernel(tc, hidden_states, gate_proj, world_size, out):
                 a = work.tile([P, 2 * P], F32, name="acc_h%d" % h, tag="acc_h%d" % h, bufs=1)
                 nc.vector.tensor_copy(out=a[:], in_=acc[jt][:, h * 2 * P : (h + 1) * 2 * P])
                 halves.append(a)
+            epi_trans(jt - 1)
+            epi_out(jt - 1)
             banks = []
             for h in range(2):
                 t = psum_t.tile([P, 2, P], F32, name="tpo_h", tag="tp")
@@ -192,8 +197,8 @@ def tile_testmmrsmodel_t_kernel(tc, hidden_states, gate_proj, world_size, out):
                     nc.tensor.transpose(t[:, i, :], halves[h][:, i * P : (i + 1) * P], ident[:])
                 banks.append(t)
             o0 = work.tile([P, 2, P], F32, name="out_h0", tag="out_h0", bufs=1)
-            nc.scalar.copy(out=o0[:], in_=banks[0][:])
-            nc.scalar.dma_start(out=dst[:, 0:2, :], in_=o0[:])
+            nc.vector.tensor_copy(out=o0[:], in_=banks[0][:])
+            nc.sync.dma_start(out=dst[:, 0:2, :], in_=o0[:])
             o1 = work.tile([P, 2, P], F32, name="out_h1", tag="out_h1", bufs=1)
             nc.vector.tensor_copy(out=o1[:], in_=banks[1][:])
             nc.sync.dma_start(out=dst[:, 2:4, :], in_=o1[:])
@@ -211,6 +216,8 @@ def tile_testmmrsmodel_t_kernel(tc, hidden_states, gate_proj, world_size, out):
                 epi_trans(jt)
             if 0 <= s + 1 < NCH:
                 evac(s + 1, "S")
+            if s + 1 == NCH - 1:
+                epi_acc(NJ - 2)
             for jt in at_out.get(s, []):
                 epi_out(jt)
             if 0 <= s + 1 < NCH:
@@ -234,7 +241,7 @@ def tile_testmmrsmodel_t_kernel(tc, hidden_states, gate_proj, world_size, out):
                         jt = c // RANKS
                         if jt == NJ - 1:
                             epi_last(jt)
-                        else:
+                        elif jt < NJ - 2:
                             at_acc[s + 1] = [jt]
                             at_trans[s + 2] = [jt]
                             at_out[s + 3] = [jt]

@@ -22,7 +22,7 @@ NCH = NJ * RANKS
 LAG = 4
 PLEAD = 4
 TLEAD = 2
-GROUP = 2
+GROUP = 1
 
 
 def is_perm(c):

@@ -55,6 +55,9 @@ def tile_testmmrsmodel_t_kernel(tc, hidden_states, gate_proj, world_size, out):
         acc_sb = {}
         tpo = {}
 
+        gate_sb = keep.tile([P, 512], BF16, name="gate_sb", tag="gate_sb")
+        nc.scalar.dma_start(out=gate_sb[:], in_=gate_proj)
+
         warm_in = keep.tile([P, 1], F32, name="warm_in", tag="warm_in")
         warm_out = keep.tile([P, 1], F32, name="warm_out", tag="warm_out")
         nc.vector.memset(warm_in[:], 0.0)
@@ -63,7 +66,6 @@ def tile_testmmrsmodel_t_kernel(tc, hidden_states, gate_proj, world_size, out):
         ident = keep.tile([P, P], F32, name="ident", tag="ident")
         make_identity(nc, ident[:])
 
-        gate_sb = keep.tile([P, 512], BF16, name="gate_sb", tag="gate_sb")
         for c in range(NCH):
             row0 = (c % RANKS) * ROWS + (c // RANKS) * CHUNK
             xt = keep.tile([P, SUB * 512], BF16, name="x%d" % c, tag="x%d" % c)
@@ -72,8 +74,6 @@ def tile_testmmrsmodel_t_kernel(tc, hidden_states, gate_proj, world_size, out):
                 in_=view[row0 : row0 + CHUNK, :].rearrange("(p i) k -> p (i k)", i=SUB),
             )
             x[c] = xt
-            if c == 1:
-                nc.sync.dma_start(out=gate_sb[:], in_=gate_proj)
 
         gate_q = keep.tile([P, P, 4], BF16, name="gate_q", tag="gate_q", align_bytes=64)
         gate_codes = keep.tile([P, P], U32, name="gate_codes", tag="gate_codes", align_bytes=64)

@@ -23,14 +23,19 @@ LAG = 4
 PLEAD = 4
 TLEAD = 2
 GROUP = 1
+VTAIL = 32
+DEFER_FROM = 99
+SPLITQ = True
+CODE_BUFS = 8
+PERM_END = 32
 
 
 def is_perm(c):
-    return c >= 8 and (c % 2 == 0 or c % 6 == 1)
+    return 8 <= c < PERM_END and (c % 2 == 0 or c % 6 == 1)
 
 
 def evac_engine(c, b):
-    return "V" if (b == 1 and (c % 8 == 0 or c == NCH - 1)) else "S"
+    return "V" if (b == 1 and (c % 8 == 0 or c >= VTAIL)) else "S"
 
 
 def tile_testmmrsmodel_t_kernel(tc, hidden_states, gate_proj, world_size, out):
@@ -136,13 +141,17 @@ def tile_testmmrsmodel_t_kernel(tc, hidden_states, gate_proj, world_size, out):
                     nc.vector.tensor_copy(out=dst, in_=src)
 
         def quant(c):
-            cd = work.tile([P, CHUNK], U32, name="codes", tag="codes", bufs=8, align_bytes=64)
-            sc = work.tile([P, CHUNK], U8, name="scales", tag="scales", bufs=8, align_bytes=64)
-            nc.vector.quantize_mx(
-                out=cd[:].bitcast(E5M2X4),
-                scales=sc[:],
-                in_=gq[c][:].rearrange("m i p t -> m (i p t)"),
-            )
+            cd = work.tile([P, CHUNK], U32, name="codes", tag="codes", bufs=CODE_BUFS, align_bytes=64)
+            sc = work.tile([P, CHUNK], U8, name="scales", tag="scales", bufs=CODE_BUFS, align_bytes=64)
+            flat = gq[c][:].rearrange("m i p t -> m (i p t)")
+            parts = 2 if (SPLITQ and c == NCH - 1) else 1
+            w = CHUNK // parts
+            for h in range(parts):
+                nc.vector.quantize_mx(
+                    out=cd[:, h * w : (h + 1) * w].bitcast(E5M2X4),
+                    scales=sc[:, h * w : (h + 1) * w],
+                    in_=flat[:, h * 4 * w : (h + 1) * 4 * w],
+                )
             codes[c] = cd
             scales[c] = sc
 
@@ -232,7 +241,7 @@ def tile_testmmrsmodel_t_kernel(tc, hidden_states, gate_proj, world_size, out):
                 perm(s + PLEAD)
             draining = s + TLEAD >= NCH - 1
             if draining or (s + 1) % GROUP == 0:
-                hi = min(NCH - 1, s if draining else s - LAG)
+                hi = min(NCH - 1, s if draining else min(s, DEFER_FROM - 1) - LAG)
                 while state["next_mm"] <= hi:
                     c = state["next_mm"]
                     state["next_mm"] = c + 1

@@ -28,6 +28,8 @@ DEFER_FROM = 99
 SPLITQ = True
 CODE_BUFS = 8
 PERM_END = 32
+VEXTRA = ()
+FINE = ("S", "S", "S", "S")
 
 
 def is_perm(c):
@@ -35,7 +37,7 @@ def is_perm(c):
 
 
 def evac_engine(c, b):
-    return "V" if (b == 1 and (c % 8 == 0 or c >= VTAIL)) else "S"
+    return "V" if (b == 1 and (c % 8 == 0 or c >= VTAIL or c in VEXTRA)) else "S"
 
 
 def tile_testmmrsmodel_t_kernel(tc, hidden_states, gate_proj, world_size, out):
@@ -113,6 +115,14 @@ def tile_testmmrsmodel_t_kernel(tc, hidden_states, gate_proj, world_size, out):
         def trans(c):
             xw = x[c][:].bitcast(F32)
             banks = []
+            if c == NCH - 1:
+                for i in range(SUB):
+                    t = psum_t.tile([P, 2, 2, P], F32, name="tp", tag="tp")
+                    for u in range(2):
+                        nc.tensor.transpose(t[:, 0, u, :], pw[c][:, u, i, :], ident[:])
+                    banks.append(t)
+                tp[c] = banks
+                return
             for b in range(2):
                 t = psum_t.tile([P, 2, 2, P], F32, name="tp", tag="tp")
                 for a in range(2):
@@ -130,6 +140,17 @@ def tile_testmmrsmodel_t_kernel(tc, hidden_states, gate_proj, world_size, out):
             if c not in gq:
                 gq[c] = work.tile([P, SUB, P, 4], BF16, name="gq", tag="gq", bufs=4, align_bytes=64)
             gw = gq[c][:].bitcast(F32)
+            if c == NCH - 1:
+                for i in range(SUB):
+                    if FINE[i] != eng:
+                        continue
+                    dst = gw[:, i : i + 1, :, :]
+                    src = tp[c][i][:, 0:1, :, :].rearrange("m a u p -> m a p u")
+                    if eng == "S":
+                        nc.scalar.copy(out=dst, in_=src)
+                    else:
+                        nc.vector.tensor_copy(out=dst, in_=src)
+                return
             for b in range(2):
                 if evac_engine(c, b) != eng:
                     continue
@@ -144,7 +165,7 @@ def tile_testmmrsmodel_t_kernel(tc, hidden_states, gate_proj, world_size, out):
             cd = work.tile([P, CHUNK], U32, name="codes", tag="codes", bufs=CODE_BUFS, align_bytes=64)
             sc = work.tile([P, CHUNK], U8, name="scales", tag="scales", bufs=CODE_BUFS, align_bytes=64)
             flat = gq[c][:].rearrange("m i p t -> m (i p t)")
-            parts = 2 if (SPLITQ and c == NCH - 1) else 1
+            parts = SUB if (SPLITQ and c == NCH - 1) else 1
             w = CHUNK // parts
             for h in range(parts):
                 nc.vector.quantize_mx(
@@ -229,12 +250,14 @@ def tile_testmmrsmodel_t_kernel(tc, hidden_states, gate_proj, world_size, out):
                 epi_acc(NJ - 2)
             for jt in at_out.get(s, []):
                 epi_out(jt)
-            if 0 <= s + 1 < NCH:
+            if 0 <= s + 1 < NCH - 1:
                 evac(s + 1, "V")
             if s + TLEAD == 1:
                 gate_quant()
             if 0 <= s < NCH:
                 quant(s)
+            if s + 1 == NCH - 1:
+                evac(s + 1, "V")
             for jt in at_acc.get(s, []):
                 epi_acc(jt)
             if 0 <= s + PLEAD < NCH and is_perm(s + PLEAD):

from contextlib import ExitStack

import concourse.mybir as mybir
from concourse.masks import make_identity

FLOPS = 2 * 16384 * 512 * 128

F32 = mybir.dt.float32
BF16 = mybir.dt.bfloat16
U32 = mybir.dt.uint32
U8 = mybir.dt.uint8
E5M2X4 = mybir.dt.float8_e5m2_x4
E4M3X4 = mybir.dt.float8_e4m3fn_x4

P = 128
RANKS = 8
ROWS = 2048
CHUNK = 512
SUB = CHUNK // P
NJ = ROWS // CHUNK
NCH = NJ * RANKS
LAG = 4
PLEAD = 4
TLEAD = 2
GROUP = 1
VTAIL = 32
DEFER_FROM = 99
SPLITQ = True
CODE_BUFS = 8
PERM_END = 32
VEXTRA = ()
FINE = ("S", "S", "S", "S")


def is_perm(c):
    return 8 <= c < PERM_END and (c % 2 == 0 or c % 6 == 1)


def evac_engine(c, b):
    return "V" if (b == 1 and (c % 8 == 0 or c >= VTAIL or c in VEXTRA)) else "S"


def tile_testmmrsmodel_t_kernel(tc, hidden_states, gate_proj, world_size, out):
    nc = tc.nc
    assert world_size == RANKS
    view = hidden_states.flatten_outer_dims()

    with ExitStack() as ctx:
        keep = ctx.enter_context(tc.tile_pool(name="keep", bufs=1))
        work = ctx.enter_context(tc.tile_pool(name="work", bufs=3))
        psum_t = ctx.enter_context(tc.psum_pool(name="psum_t", bufs=6))
        psum_a = ctx.enter_context(tc.psum_pool(name="psum_a", bufs=2))
        ctx.enter_context(tc.manual_schedule())

        x = {}
        pw = {}
        tp = {}
        gq = {}
        codes = {}
        scales = {}
        acc = {}
        acc_sb = {}
        tpo = {}

        gate_sb = keep.tile([P, 512], BF16, name="gate_sb", tag="gate_sb")
        nc.scalar.dma_start(out=gate_sb[:], in_=gate_proj)

        warm_in = keep.tile([P, 1], F32, name="warm_in", tag="warm_in")
        warm_out = keep.tile([P, 1], F32, name="warm_out", tag="warm_out")
        nc.vector.memset(warm_in[:], 0.0)
        nc.scalar.copy(out=warm_out[:], in_=warm_in[:])

        ident = keep.tile([P, P], F32, name="ident", tag="ident")
        make_identity(nc, ident[:])

        for c in range(NCH):
            row0 = (c % RANKS) * ROWS + (c // RANKS) * CHUNK
            xt = keep.tile([P, SUB * 512], BF16, name="x%d" % c, tag="x%d" % c)
            nc.sync.dma_start(
                out=xt[:],
                in_=view[row0 : row0 + CHUNK, :].rearrange("(p i) k -> p (i k)", i=SUB),
            )
            x[c] = xt

        gate_q = keep.tile([P, P, 4], BF16, name="gate_q", tag="gate_q", align_bytes=64)
        gate_codes = keep.tile([P, P], U32, name="gate_codes", tag="gate_codes", align_bytes=64)
        gate_scales = keep.tile([P, P], U8, name="gate_scales", tag="gate_scales", align_bytes=64)
        gate_bank = {}

        def gate_trans():
            gate_w = gate_sb[:].bitcast(F32)
            tg = psum_t.tile([P, 2, 2, P], F32, name="tg", tag="tp")
            for u in range(2):
                nc.tensor.transpose(tg[:, 0, u, :], gate_w[:, u:256:2], ident[:])
            gate_bank[0] = tg

        def gate_quant():
            nc.vector.tensor_copy(
                out=gate_q[:].bitcast(F32), in_=gate_bank[0][:, 0, :, :].rearrange("m u o -> m o u")
            )
            nc.vector.quantize_mx(
                out=gate_codes[:].bitcast(E4M3X4),
                scales=gate_scales[:],
                in_=gate_q[:].rearrange("m o t -> m (o t)"),
            )

        def perm(c):
            t = work.tile([P, 2, SUB, P], F32, name="pw", tag="pw", bufs=6)
            nc.vector.tensor_copy(
                out=t[:],
                in_=x[c][:].bitcast(F32).rearrange("p (i m u) -> p u i m", i=SUB, u=2),
            )
            pw[c] = t

        def trans(c):
            xw = x[c][:].bitcast(F32)
            banks = []
            if c == NCH - 1:
                for i in range(SUB):
                    t = psum_t.tile([P, 2, 2, P], F32, name="tp", tag="tp")
                    for u in range(2):
                        nc.tensor.transpose(t[:, 0, u, :], pw[c][:, u, i, :], ident[:])
                    banks.append(t)
                tp[c] = banks
                return
            for b in range(2):
                t = psum_t.tile([P, 2, 2, P], F32, name="tp", tag="tp")
                for a in range(2):
                    i = 2 * b + a
                    for u in range(2):
                        if is_perm(c):
                            src = pw[c][:, u, i, :]
                        else:
                            src = xw[:, i * 256 + u : (i + 1) * 256 : 2]
                        nc.tensor.transpose(t[:, a, u, :], src, ident[:])
                banks.append(t)
            tp[c] = banks

        def evac(c, eng):
            if c not in gq:
                gq[c] = work.tile([P, SUB, P, 4], BF16, name="gq", tag="gq", bufs=4, align_bytes=64)
            gw = gq[c][:].bitcast(F32)
            if c == NCH - 1:
                for i in range(SUB):
                    if FINE[i] != eng:
                        continue
                    dst = gw[:, i : i + 1, :, :]
                    src = tp[c][i][:, 0:1, :, :].rearrange("m a u p -> m a p u")
                    if eng == "S":
                        nc.scalar.copy(out=dst, in_=src)
                    else:
                        nc.vector.tensor_copy(out=dst, in_=src)
                return
            for b in range(2):
                if evac_engine(c, b) != eng:
                    continue
                dst = gw[:, 2 * b : 2 * b + 2, :, :]
                src = tp[c][b][:].rearrange("m a u p -> m a p u")
                if eng == "S":
                    nc.scalar.copy(out=dst, in_=src)
                else:
                    nc.vector.tensor_copy(out=dst, in_=src)

        def quant(c):
            cd = work.tile([P, CHUNK], U32, name="codes", tag="codes", bufs=CODE_BUFS, align_bytes=64)
            sc = work.tile([P, CHUNK], U8, name="scales", tag="scales", bufs=CODE_BUFS, align_bytes=64)
            flat = gq[c][:].rearrange("m i p t -> m (i p t)")
            parts = SUB if (SPLITQ and c == NCH - 1) else 1
            w = CHUNK // parts
            for h in range(parts):
                nc.vector.quantize_mx(
                    out=cd[:, h * w : (h + 1) * w].bitcast(E5M2X4),
                    scales=sc[:, h * w : (h + 1) * w],
                    in_=flat[:, h * 4 * w : (h + 1) * 4 * w],
                )
            codes[c] = cd
            scales[c] = sc

        def mm(c):
            jt = c // RANKS
            r = c % RANKS
            if r == 0:
                acc[jt] = psum_a.tile([P, CHUNK], F32, name="acc", tag="acc")
            nc.tensor.matmul_mx(
                out=acc[jt][:],
                lhsT=gate_codes[:].bitcast(E4M3X4),
                lhsT_scale=gate_scales[:],
                rhs=codes[c][:].bitcast(E5M2X4),
                rhs_scale=scales[c][:],
                start=(r == 0),
                stop=(r == RANKS - 1),
            )

        def epi_acc(jt):
            t = work.tile([P, CHUNK], F32, name="acc_sb", tag="acc_sb", bufs=2)
            if jt == NJ - 2:
                nc.scalar.copy(out=t[:], in_=acc[jt][:])
            else:
                nc.vector.tensor_copy(out=t[:], in_=acc[jt][:])
            acc_sb[jt] = t

        def epi_trans(jt):
            t = psum_t.tile([P, SUB, P], F32, name="tpo", tag="tp")
            for i in range(SUB):
                nc.tensor.transpose(t[:, i, :], acc_sb[jt][:, i * P : (i + 1) * P], ident[:])
            tpo[jt] = t

        def epi_out(jt):
            t = work.tile([P, SUB, P], F32, name="out_sb", tag="out_sb", bufs=2)
            nc.scalar.copy(out=t[:], in_=tpo[jt][:])
            dst = out[jt * CHUNK : (jt + 1) * CHUNK, :].rearrange("(p i) o -> p i o", i=SUB)
            nc.scalar.dma_start(out=dst, in_=t[:])

        def epi_last(jt):
            dst = out[jt * CHUNK : (jt + 1) * CHUNK, :].rearrange("(p i) o -> p i o", i=SUB)
            halves = []
            for h in range(2):
                a = work.tile([P, 2 * P], F32, name="acc_h%d" % h, tag="acc_h%d" % h, bufs=1)
                nc.vector.tensor_copy(out=a[:], in_=acc[jt][:, h * 2 * P : (h + 1) * 2 * P])
                halves.append(a)
            epi_trans(jt - 1)
            epi_out(jt - 1)
            banks = []
            for h in range(2):
                t = psum_t.tile([P, 2, P], F32, name="tpo_h", tag="tp")
                for i in range(2):
                    nc.tensor.transpose(t[:, i, :], halves[h][:, i * P : (i + 1) * P], ident[:])
                banks.append(t)
            o0 = work.tile([P, 2, P], F32, name="out_h0", tag="out_h0", bufs=1)
            nc.vector.tensor_copy(out=o0[:], in_=banks[0][:])
            nc.sync.dma_start(out=dst[:, 0:2, :], in_=o0[:])
            o1 = work.tile([P, 2, P], F32, name="out_h1", tag="out_h1", bufs=1)
            nc.vector.tensor_copy(out=o1[:], in_=banks[1][:])
            nc.sync.dma_start(out=dst[:, 2:4, :], in_=o1[:])

        at_acc = {}
        at_trans = {}
        at_out = {}
        state = {"next_mm": 0}
        for s in range(-PLEAD, NCH + LAG + GROUP):
            if 0 <= s + TLEAD < NCH:
                trans(s + TLEAD)
            if s + TLEAD == 1:
                gate_trans()
            for jt in at_trans.get(s, []):
                epi_trans(jt)
            if 0 <= s + 1 < NCH:
                evac(s + 1, "S")
            if s + 1 == NCH - 1:
                epi_acc(NJ - 2)
            for jt in at_out.get(s, []):
                epi_out(jt)
            if 0 <= s + 1 < NCH - 1:
                evac(s + 1, "V")
            if s + TLEAD == 1:
                gate_quant()
            if 0 <= s < NCH:
                quant(s)
            if s + 1 == NCH - 1:
                evac(s + 1, "V")
            for jt in at_acc.get(s, []):
                epi_acc(jt)
            if 0 <= s + PLEAD < NCH and is_perm(s + PLEAD):
                perm(s + PLEAD)
            draining = s + TLEAD >= NCH - 1
            if draining or (s + 1) % GROUP == 0:
                hi = min(NCH - 1, s if draining else min(s, DEFER_FROM - 1) - LAG)
                while state["next_mm"] <= hi:
                    c = state["next_mm"]
                    state["next_mm"] = c + 1
                    mm(c)
                    if c % RANKS == RANKS - 1:
                        jt = c // RANKS
                        if jt == NJ - 1:
                            epi_last(jt)
                        elif jt < NJ - 2:
                            at_acc[s + 1] = [jt]
                            at_trans[s + 2] = [jt]
                            at_out[s + 3] = [jt]
